import numpy as np
import ml_dtypes


def mxq(x, axis, fmt="e4m3"):
    dtype, down = {"e4m3": (ml_dtypes.float8_e4m3fn, 7), "e5m2": (ml_dtypes.float8_e5m2, 14)}[fmt]
    v = np.moveaxis(np.asarray(x, np.float32).astype(ml_dtypes.bfloat16).astype(np.float64), axis, -1)
    blocks = v.reshape(v.shape[:-1] + (-1, 32))
    amax = np.abs(blocks).max(-1, keepdims=True)
    byte = np.maximum(np.where(amax > 0, np.frexp(amax)[1] - 1 + 127, 0) - down, 1)
    scale = np.exp2(byte - 127.0)
    codes = (blocks / scale).astype(np.float32).astype(dtype).astype(np.float64)
    return np.moveaxis((codes * scale).reshape(v.shape), -1, axis)


WIDE = False


def mx_kscale(k):
    if not WIDE:
        return np.ones(k)
    levels = np.array([10, -10, 5, -5, 0])
    if k % 512:
        return np.exp2(np.random.permutation(np.resize(levels, k // 32))).repeat(32)
    a = np.empty((k // 512, 16))
    for p in range(k // 512):
        a[p, :8] = np.random.permutation(np.resize(levels, 8))
        for g in range(8):
            far = levels[np.abs(levels - a[p, g]) >= 10]
            a[p, g + 8] = far[np.random.randint(len(far))]
    return np.exp2(a.ravel()).repeat(32)


BF16 = ml_dtypes.bfloat16


def bf(x):
    return np.asarray(x, np.float32).astype(BF16)


def f64(x):
    return np.asarray(x).astype(np.float64)


B, N, D, A = 4, 4096, 256, 128
K = D + D
NB = N // A


def setup_inputs():
    st = mx_kscale(K)
    s, t = st[:D], st[D:]
    return {"data": bf(np.random.standard_normal((B, N, D)) * 2.0 * s),
            "pooled": bf(np.random.standard_normal((B, N, A)) * 0.37 / np.sqrt(NB)),
            "W_abs": bf(np.random.standard_normal((A, D)) * 3.0 * np.sqrt(NB / A) * t),
            "W_merge": bf(np.random.standard_normal((K, D)) * 0.5 / np.sqrt(D) / st[:, None])}


def reference(data, pooled, W_abs, W_merge):
    abstract = f64(pooled) @ f64(W_abs)
    x = np.concatenate([f64(data), abstract], axis=-1)
    return mxq(x, 2, "e4m3") @ mxq(f64(W_merge), 0, "e4m3")

@@ -1,0 +1,187 @@
+from contextlib import ExitStack
+
+import concourse.mybir as mybir
+from concourse.masks import make_identity
+
+BF16 = mybir.dt.bfloat16
+F32 = mybir.dt.float32
+U32 = mybir.dt.uint32
+U8 = mybir.dt.uint8
+FP8X4 = mybir.dt.float8_e4m3fn_x4
+
+P = 128
+PACK = 4
+TOKENS = 4 * 4096
+D = 256
+HALF_WORDS = D // 4
+A = 128
+TILES = TOKENS // P
+BANK_TILES = 2
+ROUND_TILES = 4
+ROUND_BANKS = ROUND_TILES // BANK_TILES
+ROUND_COLS = ROUND_TILES * P
+ROUNDS = TILES // ROUND_TILES
+LOAD_TILES = 8
+STORE_TILES = 8
+MERGE_LAG = 4
+
+FLOPS = 2 * TOKENS * A * D + 2 * TOKENS * (2 * D) * D
+
+
+def tile_abstraction_pb_t_kernel(tc, data, pooled, W_abs, W_merge, out):
+    nc = tc.nc
+    data_v = data.flatten_outer_dims().rearrange("(q j) d -> q j d", j=TILES)
+    pooled_v = pooled.flatten_outer_dims().rearrange("(q j) a -> q j a", j=TILES)
+    out_v = out.flatten_outer_dims().rearrange("(q j) d -> q j d", j=TILES)
+
+    with ExitStack() as stack:
+        keep = stack.enter_context(tc.tile_pool(name="keep", bufs=1))
+        work = stack.enter_context(tc.tile_pool(name="work", bufs=3))
+        quant = stack.enter_context(tc.tile_pool(name="quant", bufs=4))
+        results = stack.enter_context(tc.tile_pool(name="results", bufs=5))
+        psum_t = stack.enter_context(tc.psum_pool(name="psum_t", bufs=1))
+        psum_a = stack.enter_context(tc.psum_pool(name="psum_a", bufs=1))
+        psum_x = stack.enter_context(tc.psum_pool(name="psum_x", bufs=3))
+        psum_o = stack.enter_context(tc.psum_pool(name="psum_o", bufs=3))
+        stack.enter_context(tc.manual_schedule())
+
+        w_abs_sb = keep.tile([P, D], BF16, name="w_abs_sb")
+        nc.sync.dma_start(out=w_abs_sb[:], in_=W_abs)
+        w_raw = keep.tile([P, PACK, D], BF16, name="w_raw")
+        pooled_sb = []
+        data_sb = []
+        for c in range(TILES // LOAD_TILES):
+            tiles = slice(c * LOAD_TILES, (c + 1) * LOAD_TILES)
+            pooled_c = keep.tile([P, LOAD_TILES, A], BF16, name="pooled%d" % c)
+            nc.sync.dma_start(out=pooled_c[:], in_=pooled_v[:, tiles, :])
+            pooled_sb.append(pooled_c)
+            data_c = keep.tile([P, LOAD_TILES, D], BF16, name="data%d" % c)
+            nc.sync.dma_start(out=data_c[:], in_=data_v[:, tiles, :])
+            data_sb.append(data_c)
+            if c == 0:
+                nc.sync.dma_start(out=w_raw[:], in_=W_merge.rearrange("(p t) n -> p t n", t=PACK))
+
+        ident = keep.tile([P, P], BF16, name="ident")
+        make_identity(nc, ident[:])
+        ident_words = keep.tile([P, P], F32, name="ident_words")
+        make_identity(nc, ident_words[:])
+
+        w_abs_split = keep.tile([P, 2, HALF_WORDS, 2], BF16, name="w_abs_split")
+        nc.vector.tensor_copy(
+            out=w_abs_split[:],
+            in_=w_abs_sb[:].rearrange("p (w u e) -> p u w e", u=2, e=2),
+        )
+
+        w_grouped = keep.tile([P, D, PACK], BF16, name="w_grouped", align_bytes=64)
+        w_codes = keep.tile([P, D], U32, name="w_codes", align_bytes=64)
+        w_scales = keep.tile([P, D], U8, name="w_scales", align_bytes=64)
+
+        def prepare_w_merge():
+            nc.vector.tensor_copy(out=w_grouped[:], in_=w_raw[:].rearrange("p t n -> p n t"))
+            nc.vector.quantize_mx(
+                out=w_codes[:].bitcast(FP8X4),
+                scales=w_scales[:],
+                in_=w_grouped[:].rearrange("p n t -> p (n t)"),
+            )
+
+        pooled_t = {}
+        x = {}
+        grouped = {}
+        codes = {}
+        scales = {}
+        result = {}
+
+        def transpose_pooled(r):
+            bank = psum_t.tile([P, ROUND_TILES, P], BF16, name="pooled_bank")
+            for i in range(ROUND_TILES):
+                j = r * ROUND_TILES + i
+                nc.tensor.transpose(bank[:, i, :], pooled_sb[j // LOAD_TILES][:, j % LOAD_TILES, :], ident[:])
+            pooled_t[r] = work.tile([P, ROUND_TILES, P], BF16, name="pooled_t")
+            nc.scalar.copy(out=pooled_t[r][:], in_=bank[:])
+
+        def split_data(r):
+            x[r] = work.tile([P, ROUND_TILES, 2, 2, 2 * HALF_WORDS], BF16, name="x")
+            first = r * ROUND_TILES
+            at = first % LOAD_TILES
+            nc.vector.tensor_copy(
+                out=x[r][:].bitcast(F32)[:, :, :, 0, :],
+                in_=data_sb[first // LOAD_TILES][:]
+                .bitcast(F32)[:, at : at + ROUND_TILES, :]
+                .rearrange("p i (w u) -> p i u w", u=2),
+            )
+
+        def make_abstract(r):
+            bank = psum_a.tile([P, ROUND_TILES, 2, 2 * HALF_WORDS], BF16, name="abstract_bank")
+            for i in range(ROUND_TILES):
+                nc.tensor.matmul(
+                    bank[:, i, :, :].rearrange("p u c -> p (u c)"),
+                    lhsT=pooled_t[r][:, i, :],
+                    rhs=w_abs_split[:].rearrange("p u w e -> p (u w e)"),
+                    start=True,
+                    stop=True,
+                )
+            nc.scalar.copy(out=x[r][:, :, :, 1, :], in_=bank[:])
+
+        def transpose_x(r):
+            words = x[r][:].bitcast(F32).rearrange("p i u h w -> p i u (h w)")
+            grouped[r] = work.tile([P, ROUND_COLS, PACK], BF16, name="grouped", align_bytes=64)
+            grouped_words = grouped[r][:].bitcast(F32)
+            for b in range(ROUND_BANKS):
+                bank = psum_x.tile([P, BANK_TILES, 2, P], F32, name="x_bank")
+                for i in range(BANK_TILES):
+                    for u in range(2):
+                        nc.tensor.transpose(bank[:, i, u, :], words[:, b * BANK_TILES + i, u, :], ident_words[:])
+                cols = slice(b * BANK_TILES * P, (b + 1) * BANK_TILES * P)
+                copy = nc.vector.tensor_copy if b % 2 == 0 else nc.scalar.copy
+                copy(
+                    out=grouped_words[:, cols, :].rearrange("p (i c) u -> p i c u", i=BANK_TILES),
+                    in_=bank[:].rearrange("p i u c -> p i c u"),
+                )
+
+        def quantise_x(r):
+            codes[r] = quant.tile([P, ROUND_COLS], U32, name="codes", align_bytes=64)
+            scales[r] = quant.tile([P, ROUND_COLS], U8, name="scales", align_bytes=64)
+            nc.vector.quantize_mx(
+                out=codes[r][:].bitcast(FP8X4),
+                scales=scales[r][:],
+                in_=grouped[r][:].rearrange("p c t -> p (c t)"),
+            )
+
+        def merge(r):
+            first = r * ROUND_TILES
+            s = first // STORE_TILES
+            if first % STORE_TILES == 0:
+                result[s] = results.tile([P, STORE_TILES, D], F32, name="result")
+            for b in range(ROUND_BANKS):
+                bank = psum_o.tile([P, BANK_TILES, D], F32, name="out_bank")
+                for i in range(BANK_TILES):
+                    cols = slice((b * BANK_TILES + i) * P, (b * BANK_TILES + i + 1) * P)
+                    nc.tensor.matmul_mx(
+                        out=bank[:, i, :],
+                        lhsT=codes[r][:, cols].bitcast(FP8X4),
+                        lhsT_scale=scales[r][:, cols],
+                        rhs=w_codes[:].bitcast(FP8X4),
+                        rhs_scale=w_scales[:],
+                        start=True,
+                        stop=True,
+                    )
+                copy = nc.scalar.copy if b % 2 == 0 else nc.vector.tensor_copy
+                at = first % STORE_TILES + b * BANK_TILES
+                copy(out=result[s][:, at : at + BANK_TILES, :], in_=bank[:])
+            if (first + ROUND_TILES) % STORE_TILES == 0:
+                nc.sync.dma_start(out=out_v[:, s * STORE_TILES : (s + 1) * STORE_TILES, :], in_=result[s][:])
+
+        for step in range(ROUNDS + MERGE_LAG):
+            if step < ROUNDS:
+                transpose_pooled(step)
+                split_data(step)
+            if 1 <= step <= ROUNDS:
+                make_abstract(step - 1)
+            if 2 <= step <= ROUNDS + 1:
+                transpose_x(step - 2)
+            if step == 2:
+                prepare_w_merge()
+            if step >= MERGE_LAG:
+                merge(step - MERGE_LAG)
+            if 3 <= step <= ROUNDS + 2:
+                quantise_x(step - 3)

@@ -23,7 +23,7 @@ ROUND_COLS = ROUND_TILES * P
 ROUNDS = TILES // ROUND_TILES
 LOAD_TILES = 8
 STORE_TILES = 8
-MERGE_LAG = 4
+MERGE_LAG = 6
 
 FLOPS = 2 * TOKENS * A * D + 2 * TOKENS * (2 * D) * D
 
@@ -36,7 +36,7 @@ def tile_abstraction_pb_t_kernel(tc, data, pooled, W_abs, W_merge, out):
 
     with ExitStack() as stack:
         keep = stack.enter_context(tc.tile_pool(name="keep", bufs=1))
-        work = stack.enter_context(tc.tile_pool(name="work", bufs=3))
+        work = stack.enter_context(tc.tile_pool(name="work", bufs=4))
         quant = stack.enter_context(tc.tile_pool(name="quant", bufs=4))
         results = stack.enter_context(tc.tile_pool(name="results", bufs=5))
         psum_t = stack.enter_context(tc.psum_pool(name="psum_t", bufs=1))
@@ -97,7 +97,7 @@ def tile_abstraction_pb_t_kernel(tc, data, pooled, W_abs, W_merge, out):
                 j = r * ROUND_TILES + i
                 nc.tensor.transpose(bank[:, i, :], pooled_sb[j // LOAD_TILES][:, j % LOAD_TILES, :], ident[:])
             pooled_t[r] = work.tile([P, ROUND_TILES, P], BF16, name="pooled_t")
-            nc.scalar.copy(out=pooled_t[r][:], in_=bank[:])
+            nc.vector.tensor_copy(out=pooled_t[r][:], in_=bank[:])
 
         def split_data(r):
             x[r] = work.tile([P, ROUND_TILES, 2, 2, 2 * HALF_WORDS], BF16, name="x")
@@ -120,7 +120,7 @@ def tile_abstraction_pb_t_kernel(tc, data, pooled, W_abs, W_merge, out):
                     start=True,
                     stop=True,
                 )
-            nc.scalar.copy(out=x[r][:, :, :, 1, :], in_=bank[:])
+            nc.vector.tensor_copy(out=x[r][:, :, :, 1, :], in_=bank[:])
 
         def transpose_x(r):
             words = x[r][:].bitcast(F32).rearrange("p i u h w -> p i u (h w)")
@@ -132,7 +132,7 @@ def tile_abstraction_pb_t_kernel(tc, data, pooled, W_abs, W_merge, out):
                     for u in range(2):
                         nc.tensor.transpose(bank[:, i, u, :], words[:, b * BANK_TILES + i, u, :], ident_words[:])
                 cols = slice(b * BANK_TILES * P, (b + 1) * BANK_TILES * P)
-                copy = nc.vector.tensor_copy if b % 2 == 0 else nc.scalar.copy
+                copy = nc.vector.tensor_copy if b == 0 and r % 2 == 1 else nc.scalar.copy
                 copy(
                     out=grouped_words[:, cols, :].rearrange("p (i c) u -> p i c u", i=BANK_TILES),
                     in_=bank[:].rearrange("p i u c -> p i c u"),
@@ -165,23 +165,24 @@ def tile_abstraction_pb_t_kernel(tc, data, pooled, W_abs, W_merge, out):
                         start=True,
                         stop=True,
                     )
-                copy = nc.scalar.copy if b % 2 == 0 else nc.vector.tensor_copy
+                copy = nc.scalar.copy
                 at = first % STORE_TILES + b * BANK_TILES
                 copy(out=result[s][:, at : at + BANK_TILES, :], in_=bank[:])
             if (first + ROUND_TILES) % STORE_TILES == 0:
                 nc.sync.dma_start(out=out_v[:, s * STORE_TILES : (s + 1) * STORE_TILES, :], in_=result[s][:])
 
         for step in range(ROUNDS + MERGE_LAG):
-            if step < ROUNDS:
-                transpose_pooled(step)
-                split_data(step)
+            if 5 <= step <= ROUNDS + 4:
+                quantise_x(step - 5)
             if 1 <= step <= ROUNDS:
-                make_abstract(step - 1)
-            if 2 <= step <= ROUNDS + 1:
-                transpose_x(step - 2)
-            if step == 2:
-                prepare_w_merge()
+                split_data(step - 1)
             if step >= MERGE_LAG:
                 merge(step - MERGE_LAG)
+            if 2 <= step <= ROUNDS + 1:
+                make_abstract(step - 2)
+            if step < ROUNDS:
+                transpose_pooled(step)
             if 3 <= step <= ROUNDS + 2:
-                quantise_x(step - 3)
+                transpose_x(step - 3)
+            if step == 3:
+                prepare_w_merge()

@@ -39,27 +39,28 @@ def tile_abstraction_pb_t_kernel(tc, data, pooled, W_abs, W_merge, out):
         work = stack.enter_context(tc.tile_pool(name="work", bufs=4))
         quant = stack.enter_context(tc.tile_pool(name="quant", bufs=4))
         results = stack.enter_context(tc.tile_pool(name="results", bufs=5))
-        psum_t = stack.enter_context(tc.psum_pool(name="psum_t", bufs=1))
-        psum_a = stack.enter_context(tc.psum_pool(name="psum_a", bufs=1))
-        psum_x = stack.enter_context(tc.psum_pool(name="psum_x", bufs=3))
-        psum_o = stack.enter_context(tc.psum_pool(name="psum_o", bufs=3))
+        psum = stack.enter_context(tc.psum_pool(name="psum", bufs=8))
         stack.enter_context(tc.manual_schedule())
 
         w_abs_sb = keep.tile([P, D], BF16, name="w_abs_sb")
-        nc.sync.dma_start(out=w_abs_sb[:], in_=W_abs)
         w_raw = keep.tile([P, PACK, D], BF16, name="w_raw")
-        pooled_sb = []
-        data_sb = []
-        for c in range(TILES // LOAD_TILES):
-            tiles = slice(c * LOAD_TILES, (c + 1) * LOAD_TILES)
-            pooled_c = keep.tile([P, LOAD_TILES, A], BF16, name="pooled%d" % c)
+        pooled_sb = {}
+        data_sb = {}
+        for start in [0, ROUND_TILES] + list(range(LOAD_TILES, TILES, LOAD_TILES)):
+            width = ROUND_TILES if start < LOAD_TILES else LOAD_TILES
+            tiles = slice(start, start + width)
+            pooled_c = keep.tile([P, width, A], BF16, name="pooled%d" % start)
             nc.sync.dma_start(out=pooled_c[:], in_=pooled_v[:, tiles, :])
-            pooled_sb.append(pooled_c)
-            data_c = keep.tile([P, LOAD_TILES, D], BF16, name="data%d" % c)
+            if start == 0:
+                nc.sync.dma_start(out=w_abs_sb[:], in_=W_abs)
+            data_c = keep.tile([P, width, D], BF16, name="data%d" % start)
             nc.sync.dma_start(out=data_c[:], in_=data_v[:, tiles, :])
-            data_sb.append(data_c)
-            if c == 0:
+            if start == ROUND_TILES:
                 nc.sync.dma_start(out=w_raw[:], in_=W_merge.rearrange("(p t) n -> p t n", t=PACK))
+            for at in range(0, width, ROUND_TILES):
+                r = (start + at) // ROUND_TILES
+                pooled_sb[r] = pooled_c[:, at : at + ROUND_TILES, :]
+                data_sb[r] = data_c[:].bitcast(F32)[:, at : at + ROUND_TILES, :]
 
         ident = keep.tile([P, P], BF16, name="ident")
         make_identity(nc, ident[:])
@@ -92,26 +93,21 @@ def tile_abstraction_pb_t_kernel(tc, data, pooled, W_abs, W_merge, out):
         result = {}
 
         def transpose_pooled(r):
-            bank = psum_t.tile([P, ROUND_TILES, P], BF16, name="pooled_bank")
+            bank = psum.tile([P, 2 * ROUND_TILES, P], BF16, name="bank")
             for i in range(ROUND_TILES):
-                j = r * ROUND_TILES + i
-                nc.tensor.transpose(bank[:, i, :], pooled_sb[j // LOAD_TILES][:, j % LOAD_TILES, :], ident[:])
+                nc.tensor.transpose(bank[:, i, :], pooled_sb[r][:, i, :], ident[:])
             pooled_t[r] = work.tile([P, ROUND_TILES, P], BF16, name="pooled_t")
-            nc.vector.tensor_copy(out=pooled_t[r][:], in_=bank[:])
+            nc.vector.tensor_copy(out=pooled_t[r][:], in_=bank[:, 0:ROUND_TILES, :])
 
         def split_data(r):
             x[r] = work.tile([P, ROUND_TILES, 2, 2, 2 * HALF_WORDS], BF16, name="x")
-            first = r * ROUND_TILES
-            at = first % LOAD_TILES
             nc.vector.tensor_copy(
                 out=x[r][:].bitcast(F32)[:, :, :, 0, :],
-                in_=data_sb[first // LOAD_TILES][:]
-                .bitcast(F32)[:, at : at + ROUND_TILES, :]
-                .rearrange("p i (w u) -> p i u w", u=2),
+                in_=data_sb[r].rearrange("p i (w u) -> p i u w", u=2),
             )
 
         def make_abstract(r):
-            bank = psum_a.tile([P, ROUND_TILES, 2, 2 * HALF_WORDS], BF16, name="abstract_bank")
+            bank = psum.tile([P, ROUND_TILES, 2, 2 * HALF_WORDS], BF16, name="bank")
             for i in range(ROUND_TILES):
                 nc.tensor.matmul(
                     bank[:, i, :, :].rearrange("p u c -> p (u c)"),
@@ -127,12 +123,12 @@ def tile_abstraction_pb_t_kernel(tc, data, pooled, W_abs, W_merge, out):
             grouped[r] = work.tile([P, ROUND_COLS, PACK], BF16, name="grouped", align_bytes=64)
             grouped_words = grouped[r][:].bitcast(F32)
             for b in range(ROUND_BANKS):
-                bank = psum_x.tile([P, BANK_TILES, 2, P], F32, name="x_bank")
+                bank = psum.tile([P, BANK_TILES, 2, P], F32, name="bank")
                 for i in range(BANK_TILES):
                     for u in range(2):
                         nc.tensor.transpose(bank[:, i, u, :], words[:, b * BANK_TILES + i, u, :], ident_words[:])
                 cols = slice(b * BANK_TILES * P, (b + 1) * BANK_TILES * P)
-                copy = nc.vector.tensor_copy if b == 0 and r % 2 == 1 else nc.scalar.copy
+                copy = nc.vector.tensor_copy if b == 0 and (r % 2 == 1 or r >= ROUNDS - 3) else nc.scalar.copy
                 copy(
                     out=grouped_words[:, cols, :].rearrange("p (i c) u -> p i c u", i=BANK_TILES),
                     in_=bank[:].rearrange("p i u c -> p i c u"),
@@ -153,7 +149,7 @@ def tile_abstraction_pb_t_kernel(tc, data, pooled, W_abs, W_merge, out):
             if first % STORE_TILES == 0:
                 result[s] = results.tile([P, STORE_TILES, D], F32, name="result")
             for b in range(ROUND_BANKS):
-                bank = psum_o.tile([P, BANK_TILES, D], F32, name="out_bank")
+                bank = psum.tile([P, BANK_TILES, D], F32, name="bank")
                 for i in range(BANK_TILES):
                     cols = slice((b * BANK_TILES + i) * P, (b * BANK_TILES + i + 1) * P)
                     nc.tensor.matmul_mx(
@@ -165,10 +161,13 @@ def tile_abstraction_pb_t_kernel(tc, data, pooled, W_abs, W_merge, out):
                         start=True,
                         stop=True,
                     )
-                copy = nc.scalar.copy
+                copy = nc.vector.tensor_copy if b == 0 and r >= ROUNDS - 4 else nc.scalar.copy
                 at = first % STORE_TILES + b * BANK_TILES
                 copy(out=result[s][:, at : at + BANK_TILES, :], in_=bank[:])
-            if (first + ROUND_TILES) % STORE_TILES == 0:
+                if s == TILES // STORE_TILES - 1:
+                    tiles = slice(s * STORE_TILES + at, s * STORE_TILES + at + BANK_TILES)
+                    nc.sync.dma_start(out=out_v[:, tiles, :], in_=result[s][:, at : at + BANK_TILES, :])
+            if (first + ROUND_TILES) % STORE_TILES == 0 and s < TILES // STORE_TILES - 1:
                 nc.sync.dma_start(out=out_v[:, s * STORE_TILES : (s + 1) * STORE_TILES, :], in_=result[s][:])
 
         for step in range(ROUNDS + MERGE_LAG):

@@ -128,7 +128,7 @@ def tile_abstraction_pb_t_kernel(tc, data, pooled, W_abs, W_merge, out):
                     for u in range(2):
                         nc.tensor.transpose(bank[:, i, u, :], words[:, b * BANK_TILES + i, u, :], ident_words[:])
                 cols = slice(b * BANK_TILES * P, (b + 1) * BANK_TILES * P)
-                copy = nc.vector.tensor_copy if b == 0 and (r % 2 == 1 or r >= ROUNDS - 3) else nc.scalar.copy
+                copy = nc.vector.tensor_copy if b == 0 and (3 * r % 8 < 3 or r >= ROUNDS - 3) else nc.scalar.copy
                 copy(
                     out=grouped_words[:, cols, :].rearrange("p (i c) u -> p i c u", i=BANK_TILES),
                     in_=bank[:].rearrange("p i u c -> p i c u"),

@@ -22,8 +22,10 @@ ROUND_BANKS = ROUND_TILES // BANK_TILES
 ROUND_COLS = ROUND_TILES * P
 ROUNDS = TILES // ROUND_TILES
 LOAD_TILES = 8
+LOADS = TILES // LOAD_TILES
+POOLED_AHEAD = 6
 STORE_TILES = 8
-MERGE_LAG = 6
+MERGE_LAG = 5
 
 FLOPS = 2 * TOKENS * A * D + 2 * TOKENS * (2 * D) * D
 
@@ -37,6 +39,7 @@ def tile_abstraction_pb_t_kernel(tc, data, pooled, W_abs, W_merge, out):
     with ExitStack() as stack:
         keep = stack.enter_context(tc.tile_pool(name="keep", bufs=1))
         work = stack.enter_context(tc.tile_pool(name="work", bufs=4))
+        ahead = stack.enter_context(tc.tile_pool(name="ahead", bufs=POOLED_AHEAD + 4))
         quant = stack.enter_context(tc.tile_pool(name="quant", bufs=4))
         results = stack.enter_context(tc.tile_pool(name="results", bufs=5))
         psum = stack.enter_context(tc.psum_pool(name="psum", bufs=8))
@@ -46,21 +49,32 @@ def tile_abstraction_pb_t_kernel(tc, data, pooled, W_abs, W_merge, out):
         w_raw = keep.tile([P, PACK, D], BF16, name="w_raw")
         pooled_sb = {}
         data_sb = {}
-        for start in [0, ROUND_TILES] + list(range(LOAD_TILES, TILES, LOAD_TILES)):
-            width = ROUND_TILES if start < LOAD_TILES else LOAD_TILES
-            tiles = slice(start, start + width)
-            pooled_c = keep.tile([P, width, A], BF16, name="pooled%d" % start)
-            nc.sync.dma_start(out=pooled_c[:], in_=pooled_v[:, tiles, :])
-            if start == 0:
-                nc.sync.dma_start(out=w_abs_sb[:], in_=W_abs)
-            data_c = keep.tile([P, width, D], BF16, name="data%d" % start)
-            nc.sync.dma_start(out=data_c[:], in_=data_v[:, tiles, :])
-            if start == ROUND_TILES:
-                nc.sync.dma_start(out=w_raw[:], in_=W_merge.rearrange("(p t) n -> p t n", t=PACK))
+
+        def load_pooled(start, width):
+            tile = keep.tile([P, width, A], BF16, name="pooled%d" % start)
+            nc.sync.dma_start(out=tile[:], in_=pooled_v[:, start : start + width, :])
             for at in range(0, width, ROUND_TILES):
-                r = (start + at) // ROUND_TILES
-                pooled_sb[r] = pooled_c[:, at : at + ROUND_TILES, :]
-                data_sb[r] = data_c[:].bitcast(F32)[:, at : at + ROUND_TILES, :]
+                pooled_sb[(start + at) // ROUND_TILES] = tile[:, at : at + ROUND_TILES, :]
+
+        def load_data(start, width):
+            tile = keep.tile([P, width, D], BF16, name="data%d" % start)
+            nc.sync.dma_start(out=tile[:], in_=data_v[:, start : start + width, :])
+            for at in range(0, width, ROUND_TILES):
+                data_sb[(start + at) // ROUND_TILES] = tile[:].bitcast(F32)[:, at : at + ROUND_TILES, :]
+
+        load_pooled(0, ROUND_TILES)
+        nc.sync.dma_start(out=w_abs_sb[:], in_=W_abs)
+        load_pooled(ROUND_TILES, ROUND_TILES)
+        load_data(0, ROUND_TILES)
+        load_pooled(LOAD_TILES, LOAD_TILES)
+        load_data(ROUND_TILES, ROUND_TILES)
+        nc.sync.dma_start(out=w_raw[:], in_=W_merge.rearrange("(p t) n -> p t n", t=PACK))
+        pooled_next = 2
+        for c in range(1, LOADS):
+            while pooled_next <= min(2 * c, c + POOLED_AHEAD // 2, LOADS - 1):
+                load_pooled(pooled_next * LOAD_TILES, LOAD_TILES)
+                pooled_next += 1
+            load_data(c * LOAD_TILES, LOAD_TILES)
 
         ident = keep.tile([P, P], BF16, name="ident")
         make_identity(nc, ident[:])
@@ -96,8 +110,9 @@ def tile_abstraction_pb_t_kernel(tc, data, pooled, W_abs, W_merge, out):
             bank = psum.tile([P, 2 * ROUND_TILES, P], BF16, name="bank")
             for i in range(ROUND_TILES):
                 nc.tensor.transpose(bank[:, i, :], pooled_sb[r][:, i, :], ident[:])
-            pooled_t[r] = work.tile([P, ROUND_TILES, P], BF16, name="pooled_t")
-            nc.vector.tensor_copy(out=pooled_t[r][:], in_=bank[:, 0:ROUND_TILES, :])
+            pooled_t[r] = ahead.tile([P, ROUND_TILES, P], BF16, name="pooled_t")
+            copy = nc.scalar.copy if r < 2 * POOLED_AHEAD and r % 2 == 0 else nc.vector.tensor_copy
+            copy(out=pooled_t[r][:], in_=bank[:, 0:ROUND_TILES, :])
 
         def split_data(r):
             x[r] = work.tile([P, ROUND_TILES, 2, 2, 2 * HALF_WORDS], BF16, name="x")
@@ -116,7 +131,8 @@ def tile_abstraction_pb_t_kernel(tc, data, pooled, W_abs, W_merge, out):
                     start=True,
                     stop=True,
                 )
-            nc.vector.tensor_copy(out=x[r][:, :, :, 1, :], in_=bank[:])
+            copy = nc.scalar.copy if r < 1 else nc.vector.tensor_copy
+            copy(out=x[r][:, :, :, 1, :], in_=bank[:])
 
         def transpose_x(r):
             words = x[r][:].bitcast(F32).rearrange("p i u h w -> p i u (h w)")
@@ -171,17 +187,18 @@ def tile_abstraction_pb_t_kernel(tc, data, pooled, W_abs, W_merge, out):
                 nc.sync.dma_start(out=out_v[:, s * STORE_TILES : (s + 1) * STORE_TILES, :], in_=result[s][:])
 
         for step in range(ROUNDS + MERGE_LAG):
-            if 5 <= step <= ROUNDS + 4:
-                quantise_x(step - 5)
-            if 1 <= step <= ROUNDS:
-                split_data(step - 1)
+            if 4 <= step <= ROUNDS + 3:
+                quantise_x(step - 4)
+            if step < ROUNDS:
+                split_data(step)
             if step >= MERGE_LAG:
                 merge(step - MERGE_LAG)
+            if 1 <= step <= ROUNDS:
+                make_abstract(step - 1)
+            for r in [2 * step, 2 * step + 1] if step < POOLED_AHEAD else [step + POOLED_AHEAD]:
+                if r < ROUNDS:
+                    transpose_pooled(r)
             if 2 <= step <= ROUNDS + 1:
-                make_abstract(step - 2)
-            if step < ROUNDS:
-                transpose_pooled(step)
-            if 3 <= step <= ROUNDS + 2:
-                transpose_x(step - 3)
-            if step == 3:
+                transpose_x(step - 2)
+            if step == 2:
                 prepare_w_merge()

@@ -24,7 +24,7 @@ ROUNDS = TILES // ROUND_TILES
 LOAD_TILES = 8
 LOADS = TILES // LOAD_TILES
 POOLED_AHEAD = 6
-STORE_TILES = 8
+STORE_TILES = 4
 MERGE_LAG = 5
 
 FLOPS = 2 * TOKENS * A * D + 2 * TOKENS * (2 * D) * D
@@ -41,7 +41,7 @@ def tile_abstraction_pb_t_kernel(tc, data, pooled, W_abs, W_merge, out):
         work = stack.enter_context(tc.tile_pool(name="work", bufs=4))
         ahead = stack.enter_context(tc.tile_pool(name="ahead", bufs=POOLED_AHEAD + 4))
         quant = stack.enter_context(tc.tile_pool(name="quant", bufs=4))
-        results = stack.enter_context(tc.tile_pool(name="results", bufs=5))
+        results = stack.enter_context(tc.tile_pool(name="results", bufs=12))
         psum = stack.enter_context(tc.psum_pool(name="psum", bufs=8))
         stack.enter_context(tc.manual_schedule())
 

@@ -25,7 +25,7 @@ LOAD_TILES = 8
 LOADS = TILES // LOAD_TILES
 POOLED_AHEAD = 6
 STORE_TILES = 4
-MERGE_LAG = 5
+MERGE_LAG = 6
 
 FLOPS = 2 * TOKENS * A * D + 2 * TOKENS * (2 * D) * D
 
@@ -100,6 +100,7 @@ def tile_abstraction_pb_t_kernel(tc, data, pooled, W_abs, W_merge, out):
             )
 
         pooled_t = {}
+        abstract_copy = {}
         x = {}
         grouped = {}
         codes = {}
@@ -108,11 +109,15 @@ def tile_abstraction_pb_t_kernel(tc, data, pooled, W_abs, W_merge, out):
 
         def transpose_pooled(r):
             bank = psum.tile([P, 2 * ROUND_TILES, P], BF16, name="bank")
-            for i in range(ROUND_TILES):
+
+            def one(i):
                 nc.tensor.transpose(bank[:, i, :], pooled_sb[r][:, i, :], ident[:])
-            pooled_t[r] = ahead.tile([P, ROUND_TILES, P], BF16, name="pooled_t")
-            copy = nc.scalar.copy if r < 2 * POOLED_AHEAD and r % 2 == 0 else nc.vector.tensor_copy
-            copy(out=pooled_t[r][:], in_=bank[:, 0:ROUND_TILES, :])
+                if i == ROUND_TILES - 1:
+                    pooled_t[r] = ahead.tile([P, ROUND_TILES, P], BF16, name="pooled_t")
+                    copy = nc.scalar.copy if r < 2 * POOLED_AHEAD and r % 2 == 0 else nc.vector.tensor_copy
+                    copy(out=pooled_t[r][:], in_=bank[:, 0:ROUND_TILES, :])
+
+            return [lambda i=i: one(i) for i in range(ROUND_TILES)]
 
         def split_data(r):
             x[r] = work.tile([P, ROUND_TILES, 2, 2, 2 * HALF_WORDS], BF16, name="x")
@@ -123,7 +128,8 @@ def tile_abstraction_pb_t_kernel(tc, data, pooled, W_abs, W_merge, out):
 
         def make_abstract(r):
             bank = psum.tile([P, ROUND_TILES, 2, 2 * HALF_WORDS], BF16, name="bank")
-            for i in range(ROUND_TILES):
+
+            def one(i):
                 nc.tensor.matmul(
                     bank[:, i, :, :].rearrange("p u c -> p (u c)"),
                     lhsT=pooled_t[r][:, i, :],
@@ -131,24 +137,34 @@ def tile_abstraction_pb_t_kernel(tc, data, pooled, W_abs, W_merge, out):
                     start=True,
                     stop=True,
                 )
-            copy = nc.scalar.copy if r < 1 else nc.vector.tensor_copy
-            copy(out=x[r][:, :, :, 1, :], in_=bank[:])
+            def take():
+                copy = nc.scalar.copy if r < 1 else nc.vector.tensor_copy
+                copy(out=x[r][:, :, :, 1, :], in_=bank[:])
+
+            abstract_copy[r] = take
+
+            return [lambda i=i: one(i) for i in range(ROUND_TILES)]
 
         def transpose_x(r):
             words = x[r][:].bitcast(F32).rearrange("p i u h w -> p i u (h w)")
             grouped[r] = work.tile([P, ROUND_COLS, PACK], BF16, name="grouped", align_bytes=64)
             grouped_words = grouped[r][:].bitcast(F32)
+            parts = []
             for b in range(ROUND_BANKS):
                 bank = psum.tile([P, BANK_TILES, 2, P], F32, name="bank")
-                for i in range(BANK_TILES):
-                    for u in range(2):
-                        nc.tensor.transpose(bank[:, i, u, :], words[:, b * BANK_TILES + i, u, :], ident_words[:])
-                cols = slice(b * BANK_TILES * P, (b + 1) * BANK_TILES * P)
-                copy = nc.vector.tensor_copy if b == 0 and (3 * r % 8 < 3 or r >= ROUNDS - 3) else nc.scalar.copy
-                copy(
-                    out=grouped_words[:, cols, :].rearrange("p (i c) u -> p i c u", i=BANK_TILES),
-                    in_=bank[:].rearrange("p i u c -> p i c u"),
-                )
+
+                def one(i, u, b=b, bank=bank):
+                    nc.tensor.transpose(bank[:, i, u, :], words[:, b * BANK_TILES + i, u, :], ident_words[:])
+                    if i == BANK_TILES - 1 and u == 1:
+                        cols = slice(b * BANK_TILES * P, (b + 1) * BANK_TILES * P)
+                        copy = nc.vector.tensor_copy if b == 0 and (3 * r % 8 < 3 or r >= ROUNDS - 3) else nc.scalar.copy
+                        copy(
+                            out=grouped_words[:, cols, :].rearrange("p (i c) u -> p i c u", i=BANK_TILES),
+                            in_=bank[:].rearrange("p i u c -> p i c u"),
+                        )
+
+                parts += [lambda i=i, u=u, one=one: one(i, u) for i in range(BANK_TILES) for u in range(2)]
+            return parts
 
         def quantise_x(r):
             codes[r] = quant.tile([P, ROUND_COLS], U32, name="codes", align_bytes=64)
@@ -187,18 +203,28 @@ def tile_abstraction_pb_t_kernel(tc, data, pooled, W_abs, W_merge, out):
                 nc.sync.dma_start(out=out_v[:, s * STORE_TILES : (s + 1) * STORE_TILES, :], in_=result[s][:])
 
         for step in range(ROUNDS + MERGE_LAG):
-            if 4 <= step <= ROUNDS + 3:
-                quantise_x(step - 4)
+            if 5 <= step < ROUNDS + 5:
+                quantise_x(step - 5)
+            if 2 <= step <= ROUNDS + 1:
+                abstract_copy[step - 2]()
             if step < ROUNDS:
                 split_data(step)
             if step >= MERGE_LAG:
                 merge(step - MERGE_LAG)
-            if 1 <= step <= ROUNDS:
-                make_abstract(step - 1)
+            turns = []
             for r in [2 * step, 2 * step + 1] if step < POOLED_AHEAD else [step + POOLED_AHEAD]:
                 if r < ROUNDS:
-                    transpose_pooled(r)
-            if 2 <= step <= ROUNDS + 1:
-                transpose_x(step - 2)
+                    turns += transpose_pooled(r)
+            if 3 <= step < ROUNDS + 3:
+                turns += transpose_x(step - 3)
+            products = make_abstract(step - 1) if 1 <= step <= ROUNDS else []
+            for i, product in enumerate(products):
+                product()
+                if i < ROUND_TILES - 1:
+                    for turn in turns[i * len(turns) // (ROUND_TILES - 1) : (i + 1) * len(turns) // (ROUND_TILES - 1)]:
+                        turn()
+            if not products:
+                for turn in turns:
+                    turn()
             if step == 2:
                 prepare_w_merge()

@@ -45,6 +45,13 @@ def tile_abstraction_pb_t_kernel(tc, data, pooled, W_abs, W_merge, out):
         psum = stack.enter_context(tc.psum_pool(name="psum", bufs=8))
         stack.enter_context(tc.manual_schedule())
 
+        def pooled_done(step):
+            return min(ROUNDS, step + 1 + min(6, max(0, step + 1 - 0)))
+
+        pooled_step = {}
+        for step in range(ROUNDS):
+            for r in range(pooled_done(step - 1) if step else 0, pooled_done(step)):
+                pooled_step[r] = step
         w_abs_sb = keep.tile([P, D], BF16, name="w_abs_sb")
         w_raw = keep.tile([P, PACK, D], BF16, name="w_raw")
         pooled_sb = {}
@@ -62,19 +69,20 @@ def tile_abstraction_pb_t_kernel(tc, data, pooled, W_abs, W_merge, out):
             for at in range(0, width, ROUND_TILES):
                 data_sb[(start + at) // ROUND_TILES] = tile[:].bitcast(F32)[:, at : at + ROUND_TILES, :]
 
-        load_pooled(0, ROUND_TILES)
-        nc.sync.dma_start(out=w_abs_sb[:], in_=W_abs)
-        load_pooled(ROUND_TILES, ROUND_TILES)
-        load_data(0, ROUND_TILES)
-        load_pooled(LOAD_TILES, LOAD_TILES)
-        load_data(ROUND_TILES, ROUND_TILES)
-        nc.sync.dma_start(out=w_raw[:], in_=W_merge.rearrange("(p t) n -> p t n", t=PACK))
-        pooled_next = 2
-        for c in range(1, LOADS):
-            while pooled_next <= min(2 * c, c + POOLED_AHEAD // 2, LOADS - 1):
-                load_pooled(pooled_next * LOAD_TILES, LOAD_TILES)
-                pooled_next += 1
-            load_data(c * LOAD_TILES, LOAD_TILES)
+        loads = []
+        for start, width in [(0, ROUND_TILES), (ROUND_TILES, ROUND_TILES)] + [
+            (c * LOAD_TILES, LOAD_TILES) for c in range(1, LOADS)
+        ]:
+            r = start // ROUND_TILES
+            loads.append((pooled_step[r], 0, start, load_pooled, width))
+            loads.append((r + 1, 1, start, load_data, width))
+        loads.sort(key=lambda load: load[:3])
+        for n, (step, kind, start, load, width) in enumerate(loads):
+            load(start, width)
+            if n == 0:
+                nc.sync.dma_start(out=w_abs_sb[:], in_=W_abs)
+            if n == 7:
+                nc.sync.dma_start(out=w_raw[:], in_=W_merge.rearrange("(p t) n -> p t n", t=PACK))
 
         ident = keep.tile([P, P], BF16, name="ident")
         make_identity(nc, ident[:])
@@ -207,13 +215,13 @@ def tile_abstraction_pb_t_kernel(tc, data, pooled, W_abs, W_merge, out):
                 quantise_x(step - 5)
             if 2 <= step <= ROUNDS + 1:
                 abstract_copy[step - 2]()
-            if step < ROUNDS:
-                split_data(step)
+            if 1 <= step <= ROUNDS:
+                split_data(step - 1)
             if step >= MERGE_LAG:
                 merge(step - MERGE_LAG)
             turns = []
-            for r in [2 * step, 2 * step + 1] if step < POOLED_AHEAD else [step + POOLED_AHEAD]:
-                if r < ROUNDS:
+            for r in range(ROUNDS):
+                if pooled_step[r] == step:
                     turns += transpose_pooled(r)
             if 3 <= step < ROUNDS + 3:
                 turns += transpose_x(step - 3)
@@ -226,5 +234,5 @@ def tile_abstraction_pb_t_kernel(tc, data, pooled, W_abs, W_merge, out):
             if not products:
                 for turn in turns:
                     turn()
-            if step == 2:
+            if step == 4:
                 prepare_w_merge()

from contextlib import ExitStack

import concourse.mybir as mybir
from concourse.masks import make_identity

BF16 = mybir.dt.bfloat16
F32 = mybir.dt.float32
U32 = mybir.dt.uint32
U8 = mybir.dt.uint8
FP8X4 = mybir.dt.float8_e4m3fn_x4

P = 128
PACK = 4
TOKENS = 4 * 4096
D = 256
HALF_WORDS = D // 4
A = 128
TILES = TOKENS // P
BANK_TILES = 2
ROUND_TILES = 4
ROUND_BANKS = ROUND_TILES // BANK_TILES
ROUND_COLS = ROUND_TILES * P
ROUNDS = TILES // ROUND_TILES
LOAD_TILES = 8
LOADS = TILES // LOAD_TILES
POOLED_AHEAD = 6
STORE_TILES = 4
MERGE_LAG = 6

FLOPS = 2 * TOKENS * A * D + 2 * TOKENS * (2 * D) * D


def tile_abstraction_pb_t_kernel(tc, data, pooled, W_abs, W_merge, out):
    nc = tc.nc
    data_v = data.flatten_outer_dims().rearrange("(q j) d -> q j d", j=TILES)
    pooled_v = pooled.flatten_outer_dims().rearrange("(q j) a -> q j a", j=TILES)
    out_v = out.flatten_outer_dims().rearrange("(q j) d -> q j d", j=TILES)

    with ExitStack() as stack:
        keep = stack.enter_context(tc.tile_pool(name="keep", bufs=1))
        work = stack.enter_context(tc.tile_pool(name="work", bufs=4))
        ahead = stack.enter_context(tc.tile_pool(name="ahead", bufs=POOLED_AHEAD + 4))
        quant = stack.enter_context(tc.tile_pool(name="quant", bufs=4))
        results = stack.enter_context(tc.tile_pool(name="results", bufs=12))
        psum = stack.enter_context(tc.psum_pool(name="psum", bufs=8))
        stack.enter_context(tc.manual_schedule())

        def pooled_done(step):
            return min(ROUNDS, step + 1 + min(6, max(0, step + 1 - 0)))

        pooled_step = {}
        for step in range(ROUNDS):
            for r in range(pooled_done(step - 1) if step else 0, pooled_done(step)):
                pooled_step[r] = step
        w_abs_sb = keep.tile([P, D], BF16, name="w_abs_sb")
        w_raw = keep.tile([P, PACK, D], BF16, name="w_raw")
        pooled_sb = {}
        data_sb = {}

        def load_pooled(start, width):
            tile = keep.tile([P, width, A], BF16, name="pooled%d" % start)
            nc.sync.dma_start(out=tile[:], in_=pooled_v[:, start : start + width, :])
            for at in range(0, width, ROUND_TILES):
                pooled_sb[(start + at) // ROUND_TILES] = tile[:, at : at + ROUND_TILES, :]

        def load_data(start, width):
            tile = keep.tile([P, width, D], BF16, name="data%d" % start)
            nc.sync.dma_start(out=tile[:], in_=data_v[:, start : start + width, :])
            for at in range(0, width, ROUND_TILES):
                data_sb[(start + at) // ROUND_TILES] = tile[:].bitcast(F32)[:, at : at + ROUND_TILES, :]

        loads = []
        for start, width in [(0, ROUND_TILES), (ROUND_TILES, ROUND_TILES)] + [
            (c * LOAD_TILES, LOAD_TILES) for c in range(1, LOADS)
        ]:
            r = start // ROUND_TILES
            loads.append((pooled_step[r], 0, start, load_pooled, width))
            loads.append((r + 1, 1, start, load_data, width))
        loads.sort(key=lambda load: load[:3])
        for n, (step, kind, start, load, width) in enumerate(loads):
            load(start, width)
            if n == 0:
                nc.sync.dma_start(out=w_abs_sb[:], in_=W_abs)
            if n == 7:
                nc.sync.dma_start(out=w_raw[:], in_=W_merge.rearrange("(p t) n -> p t n", t=PACK))

        ident = keep.tile([P, P], BF16, name="ident")
        make_identity(nc, ident[:])
        ident_words = keep.tile([P, P], F32, name="ident_words")
        make_identity(nc, ident_words[:])

        w_abs_split = keep.tile([P, 2, HALF_WORDS, 2], BF16, name="w_abs_split")
        nc.vector.tensor_copy(
            out=w_abs_split[:],
            in_=w_abs_sb[:].rearrange("p (w u e) -> p u w e", u=2, e=2),
        )

        w_grouped = keep.tile([P, D, PACK], BF16, name="w_grouped", align_bytes=64)
        w_codes = keep.tile([P, D], U32, name="w_codes", align_bytes=64)
        w_scales = keep.tile([P, D], U8, name="w_scales", align_bytes=64)

        def prepare_w_merge():
            nc.vector.tensor_copy(out=w_grouped[:], in_=w_raw[:].rearrange("p t n -> p n t"))
            nc.vector.quantize_mx(
                out=w_codes[:].bitcast(FP8X4),
                scales=w_scales[:],
                in_=w_grouped[:].rearrange("p n t -> p (n t)"),
            )

        pooled_t = {}
        abstract_copy = {}
        x = {}
        grouped = {}
        codes = {}
        scales = {}
        result = {}

        def transpose_pooled(r):
            bank = psum.tile([P, 2 * ROUND_TILES, P], BF16, name="bank")

            def one(i):
                nc.tensor.transpose(bank[:, i, :], pooled_sb[r][:, i, :], ident[:])
                if i == ROUND_TILES - 1:
                    pooled_t[r] = ahead.tile([P, ROUND_TILES, P], BF16, name="pooled_t")
                    copy = nc.scalar.copy if r < 2 * POOLED_AHEAD and r % 2 == 0 else nc.vector.tensor_copy
                    copy(out=pooled_t[r][:], in_=bank[:, 0:ROUND_TILES, :])

            return [lambda i=i: one(i) for i in range(ROUND_TILES)]

        def split_data(r):
            x[r] = work.tile([P, ROUND_TILES, 2, 2, 2 * HALF_WORDS], BF16, name="x")
            nc.vector.tensor_copy(
                out=x[r][:].bitcast(F32)[:, :, :, 0, :],
                in_=data_sb[r].rearrange("p i (w u) -> p i u w", u=2),
            )

        def make_abstract(r):
            bank = psum.tile([P, ROUND_TILES, 2, 2 * HALF_WORDS], BF16, name="bank")

            def one(i):
                nc.tensor.matmul(
                    bank[:, i, :, :].rearrange("p u c -> p (u c)"),
                    lhsT=pooled_t[r][:, i, :],
                    rhs=w_abs_split[:].rearrange("p u w e -> p (u w e)"),
                    start=True,
                    stop=True,
                )
            def take():
                copy = nc.scalar.copy if r < 1 else nc.vector.tensor_copy
                copy(out=x[r][:, :, :, 1, :], in_=bank[:])

            abstract_copy[r] = take

            return [lambda i=i: one(i) for i in range(ROUND_TILES)]

        def transpose_x(r):
            words = x[r][:].bitcast(F32).rearrange("p i u h w -> p i u (h w)")
            grouped[r] = work.tile([P, ROUND_COLS, PACK], BF16, name="grouped", align_bytes=64)
            grouped_words = grouped[r][:].bitcast(F32)
            parts = []
            for b in range(ROUND_BANKS):
                bank = psum.tile([P, BANK_TILES, 2, P], F32, name="bank")

                def one(i, u, b=b, bank=bank):
                    nc.tensor.transpose(bank[:, i, u, :], words[:, b * BANK_TILES + i, u, :], ident_words[:])
                    if i == BANK_TILES - 1 and u == 1:
                        cols = slice(b * BANK_TILES * P, (b + 1) * BANK_TILES * P)
                        copy = nc.vector.tensor_copy if b == 0 and (3 * r % 8 < 3 or r >= ROUNDS - 3) else nc.scalar.copy
                        copy(
                            out=grouped_words[:, cols, :].rearrange("p (i c) u -> p i c u", i=BANK_TILES),
                            in_=bank[:].rearrange("p i u c -> p i c u"),
                        )

                parts += [lambda i=i, u=u, one=one: one(i, u) for i in range(BANK_TILES) for u in range(2)]
            return parts

        def quantise_x(r):
            codes[r] = quant.tile([P, ROUND_COLS], U32, name="codes", align_bytes=64)
            scales[r] = quant.tile([P, ROUND_COLS], U8, name="scales", align_bytes=64)
            nc.vector.quantize_mx(
                out=codes[r][:].bitcast(FP8X4),
                scales=scales[r][:],
                in_=grouped[r][:].rearrange("p c t -> p (c t)"),
            )

        def merge(r):
            first = r * ROUND_TILES
            s = first // STORE_TILES
            if first % STORE_TILES == 0:
                result[s] = results.tile([P, STORE_TILES, D], F32, name="result")
            for b in range(ROUND_BANKS):
                bank = psum.tile([P, BANK_TILES, D], F32, name="bank")
                for i in range(BANK_TILES):
                    cols = slice((b * BANK_TILES + i) * P, (b * BANK_TILES + i + 1) * P)
                    nc.tensor.matmul_mx(
                        out=bank[:, i, :],
                        lhsT=codes[r][:, cols].bitcast(FP8X4),
                        lhsT_scale=scales[r][:, cols],
                        rhs=w_codes[:].bitcast(FP8X4),
                        rhs_scale=w_scales[:],
                        start=True,
                        stop=True,
                    )
                copy = nc.vector.tensor_copy if b == 0 and r >= ROUNDS - 4 else nc.scalar.copy
                at = first % STORE_TILES + b * BANK_TILES
                copy(out=result[s][:, at : at + BANK_TILES, :], in_=bank[:])
                if s == TILES // STORE_TILES - 1:
                    tiles = slice(s * STORE_TILES + at, s * STORE_TILES + at + BANK_TILES)
                    nc.sync.dma_start(out=out_v[:, tiles, :], in_=result[s][:, at : at + BANK_TILES, :])
            if (first + ROUND_TILES) % STORE_TILES == 0 and s < TILES // STORE_TILES - 1:
                nc.sync.dma_start(out=out_v[:, s * STORE_TILES : (s + 1) * STORE_TILES, :], in_=result[s][:])

        for step in range(ROUNDS + MERGE_LAG):
            if 5 <= step < ROUNDS + 5:
                quantise_x(step - 5)
            if 2 <= step <= ROUNDS + 1:
                abstract_copy[step - 2]()
            if 1 <= step <= ROUNDS:
                split_data(step - 1)
            if step >= MERGE_LAG:
                merge(step - MERGE_LAG)
            turns = []
            for r in range(ROUNDS):
                if pooled_step[r] == step:
                    turns += transpose_pooled(r)
            if 3 <= step < ROUNDS + 3:
                turns += transpose_x(step - 3)
            products = make_abstract(step - 1) if 1 <= step <= ROUNDS else []
            for i, product in enumerate(products):
                product()
                if i < ROUND_TILES - 1:
                    for turn in turns[i * len(turns) // (ROUND_TILES - 1) : (i + 1) * len(turns) // (ROUND_TILES - 1)]:
                        turn()
            if not products:
                for turn in turns:
                    turn()
            if step == 4:
                prepare_w_merge()
